import numpy as np
import ml_dtypes

BF16 = ml_dtypes.bfloat16


def bf(x):
    return np.asarray(x, np.float32).astype(BF16)


def f32(x):
    return np.asarray(x, np.float32)


def f64(x):
    return np.asarray(x).astype(np.float64)


def striped(idx):
    return np.tile(idx.reshape(-1, 16).T, (8, 1))


C, L, T, N, K = 256, 512, 32, 1024, 2
TERMS, CUT, SIG_S, SIG_T, SIG_B = 150, 6.0, 1.5, 1.5, 0.1


def erf(a):
    a = np.asarray(a, np.float64)
    c = np.clip(a, -CUT, CUT)
    term = c.copy()
    total = c.copy()
    for n in range(1, TERMS):
        term = term * 2.0 * c * c / (2.0 * n + 1.0)
        total = total + term
    val = 2.0 / np.sqrt(np.pi) * np.exp(-c * c) * total
    return np.where(np.abs(a) > CUT, np.sign(a), val)


def gelu_erf(v):
    return 0.5 * v * (1.0 + erf(v / np.sqrt(2.0)))


def setup_inputs():
    return {"scores": f32(SIG_S * np.sqrt(T) * np.random.standard_normal((C, N))), "tab": f32(SIG_T * np.random.standard_normal((C, L))), "b1": f32(SIG_B * np.random.standard_normal((C, 1))), "offs": striped(np.concatenate([np.random.permutation(L) for _ in range(K)]))}


def reference(scores, tab, b1, offs):
    idx = offs[:16].T.reshape(-1)
    bias = gelu_erf(f64(tab) + f64(b1))
    z = float(T) ** -0.5 * f64(scores) + bias[:, idx]
    z = z.reshape(C, T, T)
    z = z - z.max(axis=2, keepdims=True)
    e = np.exp(z)
    p = e / e.sum(axis=2, keepdims=True)
    return p.reshape(C, N)

@@ -1,0 +1,75 @@
+import concourse.mybir as mybir
+
+F32 = mybir.dt.float32
+U16 = mybir.dt.uint16
+ALU = mybir.AluOpType
+ACT = mybir.ActivationFunctionType
+X = mybir.AxisListType.X
+
+P = 128
+HEADS = 256
+BLOCKS = HEADS // P
+TABLE = 512
+QUERIES = 32
+KEYS = 32
+PAIRS = QUERIES * KEYS
+PIECE = TABLE
+PIECES = PAIRS // PIECE
+SCALE = KEYS ** -0.5
+
+
+def tile_flexattentioncpb_kernel(tc, scores, tab, b1, offs, out):
+    nc = tc.nc
+    with (
+        tc.tile_pool(name="held", bufs=1) as held,
+        tc.tile_pool(name="work", bufs=BLOCKS) as work,
+    ):
+        offsets = held.tile([P, PAIRS // 16], U16, name="offsets")
+        nc.sync.dma_start(offsets[:], offs)
+
+        biases = []
+        scaleds = []
+        for b in range(BLOCKS):
+            heads = slice(b * P, (b + 1) * P)
+            pre = work.tile([P, TABLE], F32, name="pre")
+            nc.sync.dma_start(pre[:], tab[heads, :])
+            shift = work.tile([P, 1], F32, name="shift")
+            nc.scalar.dma_start(shift[:], b1[heads, :])
+            raw = work.tile([P, PAIRS], F32, name="raw")
+            nc.scalar.dma_start(raw[:], scores[heads, :])
+
+            bias = work.tile([P, TABLE], F32, name="bias")
+            nc.scalar.activation(bias[:], pre[:], ACT.Gelu, bias=shift[:])
+            scaled = work.tile([P, PAIRS], F32, name="scaled")
+            nc.scalar.mul(scaled[:], raw[:], SCALE)
+            biases.append(bias)
+            scaleds.append(scaled)
+
+        for b in range(BLOCKS):
+            heads = slice(b * P, (b + 1) * P)
+            logit = work.tile([P, PAIRS], F32, name="logit")
+            for k in range(PIECES):
+                cols = slice(k * PIECE, (k + 1) * PIECE)
+                picked = biases[b][:].indirect(offsets[:, k * (PIECE // 16) : (k + 1) * (PIECE // 16)])
+                nc.vector.tensor_tensor(logit[:, cols], picked, scaleds[b][:, cols], ALU.add)
+
+            by_query = logit[:].rearrange("p (q k) -> p q k", k=KEYS)
+            top = work.tile([P, QUERIES], F32, name="top")
+            nc.vector.tensor_reduce(top[:], by_query, X, ALU.max)
+            nc.vector.tensor_tensor(
+                by_query, by_query, top[:].unsqueeze(2).to_broadcast([P, QUERIES, KEYS]), ALU.subtract
+            )
+            weight = work.tile([P, PAIRS], F32, name="weight")
+            nc.scalar.activation(weight[:], logit[:], ACT.Exp)
+            weight_by_query = weight[:].rearrange("p (q k) -> p q k", k=KEYS)
+            total = work.tile([P, QUERIES], F32, name="total")
+            nc.vector.tensor_reduce(total[:], weight_by_query, X, ALU.add)
+            inverse = work.tile([P, QUERIES], F32, name="inverse")
+            nc.vector.reciprocal(inverse[:], total[:])
+            nc.vector.tensor_tensor(
+                weight_by_query,
+                weight_by_query,
+                inverse[:].unsqueeze(2).to_broadcast([P, QUERIES, KEYS]),
+                ALU.mult,
+            )
+            nc.sync.dma_start(out[heads, :], weight[:])

@@ -15,61 +15,81 @@ KEYS = 32
 PAIRS = QUERIES * KEYS
 PIECE = TABLE
 PIECES = PAIRS // PIECE
+PIECE_QUERIES = PIECE // KEYS
 SCALE = KEYS ** -0.5
 
 
 def tile_flexattentioncpb_kernel(tc, scores, tab, b1, offs, out):
     nc = tc.nc
+    units = [(b, k) for b in range(BLOCKS) for k in range(PIECES)]
     with (
         tc.tile_pool(name="held", bufs=1) as held,
-        tc.tile_pool(name="work", bufs=BLOCKS) as work,
+        tc.tile_pool(name="tables", bufs=BLOCKS) as tables,
+        tc.tile_pool(name="work", bufs=len(units)) as work,
     ):
         offsets = held.tile([P, PAIRS // 16], U16, name="offsets")
         nc.sync.dma_start(offsets[:], offs)
 
-        biases = []
-        scaleds = []
+        pres, shifts, raws = [], [], []
         for b in range(BLOCKS):
             heads = slice(b * P, (b + 1) * P)
-            pre = work.tile([P, TABLE], F32, name="pre")
-            nc.sync.dma_start(pre[:], tab[heads, :])
-            shift = work.tile([P, 1], F32, name="shift")
+            shift = tables.tile([P, 1], F32, name="shift")
             nc.scalar.dma_start(shift[:], b1[heads, :])
-            raw = work.tile([P, PAIRS], F32, name="raw")
-            nc.scalar.dma_start(raw[:], scores[heads, :])
+            pre = tables.tile([P, TABLE], F32, name="pre")
+            nc.sync.dma_start(pre[:], tab[heads, :])
+            shifts.append(shift)
+            pres.append(pre)
+        for b, k in units:
+            raw = work.tile([P, PIECE], F32, name="raw")
+            nc.scalar.dma_start(raw[:], scores[b * P : (b + 1) * P, k * PIECE : (k + 1) * PIECE])
+            raws.append(raw)
 
-            bias = work.tile([P, TABLE], F32, name="bias")
-            nc.scalar.activation(bias[:], pre[:], ACT.Gelu, bias=shift[:])
-            scaled = work.tile([P, PAIRS], F32, name="scaled")
-            nc.scalar.mul(scaled[:], raw[:], SCALE)
-            biases.append(bias)
-            scaleds.append(scaled)
+        warm = held.tile([P, 1], F32, name="warm")
+        nc.vector.memset(warm[:], 0.0)
+        warm_gelu = held.tile([P, 1], F32, name="warm_gelu")
+        nc.scalar.activation(warm_gelu[:], warm[:], ACT.Gelu)
 
+        biases = []
         for b in range(BLOCKS):
-            heads = slice(b * P, (b + 1) * P)
-            logit = work.tile([P, PAIRS], F32, name="logit")
-            for k in range(PIECES):
-                cols = slice(k * PIECE, (k + 1) * PIECE)
-                picked = biases[b][:].indirect(offsets[:, k * (PIECE // 16) : (k + 1) * (PIECE // 16)])
-                nc.vector.tensor_tensor(logit[:, cols], picked, scaleds[b][:, cols], ALU.add)
+            bias = tables.tile([P, TABLE], F32, name="bias")
+            nc.scalar.activation(bias[:], pres[b][:], ACT.Gelu, bias=shifts[b][:])
+            biases.append(bias)
+        warm_exp = held.tile([P, 1], F32, name="warm_exp")
+        nc.scalar.activation(warm_exp[:], biases[-1][:, 0:1], ACT.Exp)
 
+        weights = []
+
+        def front(u):
+            b, k = units[u]
+            scaled = work.tile([P, PIECE], F32, name="scaled")
+            nc.scalar.mul(scaled[:], raws[u][:], SCALE)
+            logit = work.tile([P, PIECE], F32, name="logit")
+            picked = biases[b][:].indirect(offsets[:, k * (PIECE // 16) : (k + 1) * (PIECE // 16)])
+            nc.vector.tensor_tensor(logit[:], picked, scaled[:], ALU.add)
             by_query = logit[:].rearrange("p (q k) -> p q k", k=KEYS)
-            top = work.tile([P, QUERIES], F32, name="top")
+            top = work.tile([P, PIECE_QUERIES], F32, name="top")
             nc.vector.tensor_reduce(top[:], by_query, X, ALU.max)
             nc.vector.tensor_tensor(
-                by_query, by_query, top[:].unsqueeze(2).to_broadcast([P, QUERIES, KEYS]), ALU.subtract
+                by_query, by_query, top[:].unsqueeze(2).to_broadcast([P, PIECE_QUERIES, KEYS]), ALU.subtract
             )
-            weight = work.tile([P, PAIRS], F32, name="weight")
+            weight = work.tile([P, PIECE], F32, name="weight")
             nc.scalar.activation(weight[:], logit[:], ACT.Exp)
-            weight_by_query = weight[:].rearrange("p (q k) -> p q k", k=KEYS)
-            total = work.tile([P, QUERIES], F32, name="total")
-            nc.vector.tensor_reduce(total[:], weight_by_query, X, ALU.add)
-            inverse = work.tile([P, QUERIES], F32, name="inverse")
+            weights.append(weight)
+
+        def back(u):
+            b, k = units[u]
+            by_query = weights[u][:].rearrange("p (q k) -> p q k", k=KEYS)
+            total = work.tile([P, PIECE_QUERIES], F32, name="total")
+            nc.vector.tensor_reduce(total[:], by_query, X, ALU.add)
+            inverse = work.tile([P, PIECE_QUERIES], F32, name="inverse")
             nc.vector.reciprocal(inverse[:], total[:])
             nc.vector.tensor_tensor(
-                weight_by_query,
-                weight_by_query,
-                inverse[:].unsqueeze(2).to_broadcast([P, QUERIES, KEYS]),
-                ALU.mult,
+                by_query, by_query, inverse[:].unsqueeze(2).to_broadcast([P, PIECE_QUERIES, KEYS]), ALU.mult
             )
-            nc.sync.dma_start(out[heads, :], weight[:])
+            nc.sync.dma_start(out[b * P : (b + 1) * P, k * PIECE : (k + 1) * PIECE], weights[u][:])
+
+        front(0)
+        for u in range(1, len(units)):
+            front(u)
+            back(u - 1)
+        back(len(units) - 1)

@@ -29,19 +29,19 @@ def tile_flexattentioncpb_kernel(tc, scores, tab, b1, offs, out):
     ):
         offsets = held.tile([P, PAIRS // 16], U16, name="offsets")
         nc.sync.dma_start(offsets[:], offs)
-
+        queues = [nc.sync, nc.gpsimd]
         pres, shifts, raws = [], [], []
         for b in range(BLOCKS):
             heads = slice(b * P, (b + 1) * P)
             shift = tables.tile([P, 1], F32, name="shift")
-            nc.scalar.dma_start(shift[:], b1[heads, :])
+            queues[b].dma_start(shift[:], b1[heads, :])
             pre = tables.tile([P, TABLE], F32, name="pre")
-            nc.sync.dma_start(pre[:], tab[heads, :])
+            queues[b].dma_start(pre[:], tab[heads, :])
             shifts.append(shift)
             pres.append(pre)
         for b, k in units:
             raw = work.tile([P, PIECE], F32, name="raw")
-            nc.scalar.dma_start(raw[:], scores[b * P : (b + 1) * P, k * PIECE : (k + 1) * PIECE])
+            queues[b].dma_start(raw[:], scores[b * P : (b + 1) * P, k * PIECE : (k + 1) * PIECE])
             raws.append(raw)
 
         warm = held.tile([P, 1], F32, name="warm")
@@ -57,32 +57,35 @@ def tile_flexattentioncpb_kernel(tc, scores, tab, b1, offs, out):
         warm_exp = held.tile([P, 1], F32, name="warm_exp")
         nc.scalar.activation(warm_exp[:], biases[-1][:, 0:1], ACT.Exp)
 
-        weights = []
+        weights, totals = [], []
 
         def front(u):
             b, k = units[u]
             scaled = work.tile([P, PIECE], F32, name="scaled")
-            nc.scalar.mul(scaled[:], raws[u][:], SCALE)
+            nc.vector.tensor_scalar_mul(scaled[:], raws[u][:], SCALE)
             logit = work.tile([P, PIECE], F32, name="logit")
             picked = biases[b][:].indirect(offsets[:, k * (PIECE // 16) : (k + 1) * (PIECE // 16)])
             nc.vector.tensor_tensor(logit[:], picked, scaled[:], ALU.add)
-            by_query = logit[:].rearrange("p (q k) -> p q k", k=KEYS)
-            top = work.tile([P, PIECE_QUERIES], F32, name="top")
-            nc.vector.tensor_reduce(top[:], by_query, X, ALU.max)
-            nc.vector.tensor_tensor(
-                by_query, by_query, top[:].unsqueeze(2).to_broadcast([P, PIECE_QUERIES, KEYS]), ALU.subtract
+            minus_top = work.tile([P, PIECE_QUERIES], F32, name="minus_top")
+            nc.vector.tensor_reduce(
+                minus_top[:], logit[:].rearrange("p (q k) -> p q k", k=KEYS), X, ALU.max, negate=True
             )
             weight = work.tile([P, PIECE], F32, name="weight")
-            nc.scalar.activation(weight[:], logit[:], ACT.Exp)
+            total = work.tile([P, PIECE_QUERIES], F32, name="total")
+            for q in range(PIECE_QUERIES):
+                keys = slice(q * KEYS, (q + 1) * KEYS)
+                nc.scalar.activation(
+                    weight[:, keys], logit[:, keys], ACT.Exp,
+                    bias=minus_top[:, q : q + 1], accum_out=total[:, q : q + 1],
+                )
             weights.append(weight)
+            totals.append(total)
 
         def back(u):
             b, k = units[u]
             by_query = weights[u][:].rearrange("p (q k) -> p q k", k=KEYS)
-            total = work.tile([P, PIECE_QUERIES], F32, name="total")
-            nc.vector.tensor_reduce(total[:], by_query, X, ALU.add)
             inverse = work.tile([P, PIECE_QUERIES], F32, name="inverse")
-            nc.vector.reciprocal(inverse[:], total[:])
+            nc.vector.reciprocal(inverse[:], totals[u][:])
             nc.vector.tensor_tensor(
                 by_query, by_query, inverse[:].unsqueeze(2).to_broadcast([P, PIECE_QUERIES, KEYS]), ALU.mult
             )

@@ -28,21 +28,23 @@ def tile_flexattentioncpb_kernel(tc, scores, tab, b1, offs, out):
         tc.tile_pool(name="work", bufs=len(units)) as work,
     ):
         offsets = held.tile([P, PAIRS // 16], U16, name="offsets")
+        shifts = [tables.tile([P, 1], F32, name="shift") for b in range(BLOCKS)]
+        pres = [tables.tile([P, TABLE], F32, name="pre") for b in range(BLOCKS)]
+        raws = [work.tile([P, PIECE], F32, name="raw") for u in units]
+
+        def load_scores(queue, u):
+            b, k = units[u]
+            queue.dma_start(raws[u][:], scores[b * P : (b + 1) * P, k * PIECE : (k + 1) * PIECE])
+
+        nc.sync.dma_start(pres[0][:], tab[0:P, :])
+        nc.scalar.dma_start(shifts[0][:], b1[0:P, :])
+        load_scores(nc.scalar, 0)
         nc.sync.dma_start(offsets[:], offs)
-        queues = [nc.sync, nc.gpsimd]
-        pres, shifts, raws = [], [], []
-        for b in range(BLOCKS):
-            heads = slice(b * P, (b + 1) * P)
-            shift = tables.tile([P, 1], F32, name="shift")
-            queues[b].dma_start(shift[:], b1[heads, :])
-            pre = tables.tile([P, TABLE], F32, name="pre")
-            queues[b].dma_start(pre[:], tab[heads, :])
-            shifts.append(shift)
-            pres.append(pre)
-        for b, k in units:
-            raw = work.tile([P, PIECE], F32, name="raw")
-            queues[b].dma_start(raw[:], scores[b * P : (b + 1) * P, k * PIECE : (k + 1) * PIECE])
-            raws.append(raw)
+        load_scores(nc.sync, 1)
+        nc.sync.dma_start(shifts[1][:], b1[P : 2 * P, :])
+        nc.sync.dma_start(pres[1][:], tab[P : 2 * P, :])
+        load_scores(nc.sync, 2)
+        load_scores(nc.sync, 3)
 
         warm = held.tile([P, 1], F32, name="warm")
         nc.vector.memset(warm[:], 0.0)
@@ -58,9 +60,7 @@ def tile_flexattentioncpb_kernel(tc, scores, tab, b1, offs, out):
         nc.scalar.activation(warm_exp[:], biases[-1][:, 0:1], ACT.Exp)
 
         weights, totals = [], []
-
-        def front(u):
-            b, k = units[u]
+        for u, (b, k) in enumerate(units):
             scaled = work.tile([P, PIECE], F32, name="scaled")
             nc.vector.tensor_scalar_mul(scaled[:], raws[u][:], SCALE)
             logit = work.tile([P, PIECE], F32, name="logit")
@@ -81,8 +81,7 @@ def tile_flexattentioncpb_kernel(tc, scores, tab, b1, offs, out):
             weights.append(weight)
             totals.append(total)
 
-        def back(u):
-            b, k = units[u]
+        for u, (b, k) in enumerate(units):
             by_query = weights[u][:].rearrange("p (q k) -> p q k", k=KEYS)
             inverse = work.tile([P, PIECE_QUERIES], F32, name="inverse")
             nc.vector.reciprocal(inverse[:], totals[u][:])
@@ -90,9 +89,3 @@ def tile_flexattentioncpb_kernel(tc, scores, tab, b1, offs, out):
                 by_query, by_query, inverse[:].unsqueeze(2).to_broadcast([P, PIECE_QUERIES, KEYS]), ALU.mult
             )
             nc.sync.dma_start(out[b * P : (b + 1) * P, k * PIECE : (k + 1) * PIECE], weights[u][:])
-
-        front(0)
-        for u in range(1, len(units)):
-            front(u)
-            back(u - 1)
-        back(len(units) - 1)

@@ -18,74 +18,91 @@ PIECES = PAIRS // PIECE
 PIECE_QUERIES = PIECE // KEYS
 SCALE = KEYS ** -0.5
 
+UNITS = BLOCKS * PIECES
+AHEAD = 2
+
 
 def tile_flexattentioncpb_kernel(tc, scores, tab, b1, offs, out):
     nc = tc.nc
-    units = [(b, k) for b in range(BLOCKS) for k in range(PIECES)]
+
+    def dram_part(array, u):
+        b, k = divmod(u, PIECES)
+        return array[b * P : (b + 1) * P, k * PIECE : (k + 1) * PIECE]
+
     with (
         tc.tile_pool(name="held", bufs=1) as held,
         tc.tile_pool(name="tables", bufs=BLOCKS) as tables,
-        tc.tile_pool(name="work", bufs=len(units)) as work,
+        tc.tile_pool(name="work", bufs=UNITS) as work,
     ):
         offsets = held.tile([P, PAIRS // 16], U16, name="offsets")
         shifts = [tables.tile([P, 1], F32, name="shift") for b in range(BLOCKS)]
         pres = [tables.tile([P, TABLE], F32, name="pre") for b in range(BLOCKS)]
-        raws = [work.tile([P, PIECE], F32, name="raw") for u in units]
+        biases = [tables.tile([P, TABLE], F32, name="bias") for b in range(BLOCKS)]
+        raws = [work.tile([P, PIECE], F32, name="raw") for u in range(UNITS)]
+        scaleds = [work.tile([P, PIECE], F32, name="scaled") for u in range(UNITS)]
+        logits = [work.tile([P, PIECE], F32, name="logit") for u in range(UNITS)]
+        minus_tops = [work.tile([P, PIECE_QUERIES], F32, name="minus_top") for u in range(UNITS)]
+        weights = [work.tile([P, PIECE], F32, name="weight") for u in range(UNITS)]
+        totals = [work.tile([P, PIECE_QUERIES], F32, name="total") for u in range(UNITS)]
+        inverses = [work.tile([P, PIECE_QUERIES], F32, name="inverse") for u in range(UNITS)]
 
-        def load_scores(queue, u):
-            b, k = units[u]
-            queue.dma_start(raws[u][:], scores[b * P : (b + 1) * P, k * PIECE : (k + 1) * PIECE])
-
+        for b in range(BLOCKS):
+            nc.scalar.dma_start(shifts[b][:], b1[b * P : (b + 1) * P, :])
         nc.sync.dma_start(pres[0][:], tab[0:P, :])
-        nc.scalar.dma_start(shifts[0][:], b1[0:P, :])
-        load_scores(nc.scalar, 0)
         nc.sync.dma_start(offsets[:], offs)
-        load_scores(nc.sync, 1)
-        nc.sync.dma_start(shifts[1][:], b1[P : 2 * P, :])
+        nc.sync.dma_start(raws[0][:], dram_part(scores, 0))
         nc.sync.dma_start(pres[1][:], tab[P : 2 * P, :])
-        load_scores(nc.sync, 2)
-        load_scores(nc.sync, 3)
+        for u in range(1, UNITS):
+            nc.sync.dma_start(raws[u][:], dram_part(scores, u))
 
         warm = held.tile([P, 1], F32, name="warm")
         nc.vector.memset(warm[:], 0.0)
         warm_gelu = held.tile([P, 1], F32, name="warm_gelu")
         nc.scalar.activation(warm_gelu[:], warm[:], ACT.Gelu)
-
-        biases = []
         for b in range(BLOCKS):
-            bias = tables.tile([P, TABLE], F32, name="bias")
-            nc.scalar.activation(bias[:], pres[b][:], ACT.Gelu, bias=shifts[b][:])
-            biases.append(bias)
+            nc.scalar.activation(biases[b][:], pres[b][:], ACT.Gelu, bias=shifts[b][:])
         warm_exp = held.tile([P, 1], F32, name="warm_exp")
         nc.scalar.activation(warm_exp[:], biases[-1][:, 0:1], ACT.Exp)
 
-        weights, totals = [], []
-        for u, (b, k) in enumerate(units):
-            scaled = work.tile([P, PIECE], F32, name="scaled")
-            nc.vector.tensor_scalar_mul(scaled[:], raws[u][:], SCALE)
-            logit = work.tile([P, PIECE], F32, name="logit")
+        def scale(u):
+            nc.vector.tensor_scalar_mul(scaleds[u][:], raws[u][:], SCALE)
+
+        def add_bias(u):
+            b, k = divmod(u, PIECES)
             picked = biases[b][:].indirect(offsets[:, k * (PIECE // 16) : (k + 1) * (PIECE // 16)])
-            nc.vector.tensor_tensor(logit[:], picked, scaled[:], ALU.add)
-            minus_top = work.tile([P, PIECE_QUERIES], F32, name="minus_top")
+            nc.vector.tensor_tensor(logits[u][:], picked, scaleds[u][:], ALU.add)
+
+        def exponentials(u):
             nc.vector.tensor_reduce(
-                minus_top[:], logit[:].rearrange("p (q k) -> p q k", k=KEYS), X, ALU.max, negate=True
+                minus_tops[u][:], logits[u][:].rearrange("p (q k) -> p q k", k=KEYS), X, ALU.max, negate=True
             )
-            weight = work.tile([P, PIECE], F32, name="weight")
-            total = work.tile([P, PIECE_QUERIES], F32, name="total")
             for q in range(PIECE_QUERIES):
                 keys = slice(q * KEYS, (q + 1) * KEYS)
                 nc.scalar.activation(
-                    weight[:, keys], logit[:, keys], ACT.Exp,
-                    bias=minus_top[:, q : q + 1], accum_out=total[:, q : q + 1],
+                    weights[u][:, keys], logits[u][:, keys], ACT.Exp,
+                    bias=minus_tops[u][:, q : q + 1], accum_out=totals[u][:, q : q + 1],
                 )
-            weights.append(weight)
-            totals.append(total)
 
-        for u, (b, k) in enumerate(units):
+        def invert(u):
+            nc.vector.reciprocal(inverses[u][:], totals[u][:])
+
+        def divide(u):
             by_query = weights[u][:].rearrange("p (q k) -> p q k", k=KEYS)
-            inverse = work.tile([P, PIECE_QUERIES], F32, name="inverse")
-            nc.vector.reciprocal(inverse[:], totals[u][:])
             nc.vector.tensor_tensor(
-                by_query, by_query, inverse[:].unsqueeze(2).to_broadcast([P, PIECE_QUERIES, KEYS]), ALU.mult
+                by_query, by_query, inverses[u][:].unsqueeze(2).to_broadcast([P, PIECE_QUERIES, KEYS]), ALU.mult
             )
-            nc.sync.dma_start(out[b * P : (b + 1) * P, k * PIECE : (k + 1) * PIECE], weights[u][:])
+            nc.sync.dma_start(dram_part(out, u), weights[u][:])
+
+        for u in range(AHEAD):
+            scale(u)
+        for u in range(UNITS):
+            add_bias(u)
+            if u + AHEAD < UNITS:
+                scale(u + AHEAD)
+            else:
+                invert(u - AHEAD)
+            exponentials(u)
+        for u in range(UNITS):
+            divide(u)
+            if u + AHEAD < UNITS:
+                invert(u + AHEAD)

@@ -13,96 +13,111 @@ TABLE = 512
 QUERIES = 32
 KEYS = 32
 PAIRS = QUERIES * KEYS
-PIECE = TABLE
-PIECES = PAIRS // PIECE
-PIECE_QUERIES = PIECE // KEYS
 SCALE = KEYS ** -0.5
 
-UNITS = BLOCKS * PIECES
-AHEAD = 2
+GROWING = (4, 12, 16)
+assert sum(GROWING) == QUERIES and max(GROWING) * KEYS <= TABLE
+
+
+def units_of(block, sizes):
+    return [(block, sum(sizes[:i]), n) for i, n in enumerate(sizes)]
+
+
+UNITS = units_of(0, GROWING) + units_of(1, GROWING[::-1])
 
 
 def tile_flexattentioncpb_kernel(tc, scores, tab, b1, offs, out):
     nc = tc.nc
 
-    def dram_part(array, u):
-        b, k = divmod(u, PIECES)
-        return array[b * P : (b + 1) * P, k * PIECE : (k + 1) * PIECE]
+    def pairs_of(unit):
+        block, first, n = unit
+        return slice(first * KEYS, (first + n) * KEYS)
+
+    def queries_of(unit):
+        block, first, n = unit
+        return slice(first, first + n)
+
+    def heads_of(block):
+        return slice(block * P, (block + 1) * P)
+
+    def by_query(columns):
+        return columns.rearrange("p (q k) -> p q k", k=KEYS)
 
     with (
         tc.tile_pool(name="held", bufs=1) as held,
-        tc.tile_pool(name="tables", bufs=BLOCKS) as tables,
-        tc.tile_pool(name="work", bufs=UNITS) as work,
+        tc.tile_pool(name="blocks", bufs=BLOCKS) as blocks,
     ):
         offsets = held.tile([P, PAIRS // 16], U16, name="offsets")
-        shifts = [tables.tile([P, 1], F32, name="shift") for b in range(BLOCKS)]
-        pres = [tables.tile([P, TABLE], F32, name="pre") for b in range(BLOCKS)]
-        biases = [tables.tile([P, TABLE], F32, name="bias") for b in range(BLOCKS)]
-        raws = [work.tile([P, PIECE], F32, name="raw") for u in range(UNITS)]
-        scaleds = [work.tile([P, PIECE], F32, name="scaled") for u in range(UNITS)]
-        logits = [work.tile([P, PIECE], F32, name="logit") for u in range(UNITS)]
-        minus_tops = [work.tile([P, PIECE_QUERIES], F32, name="minus_top") for u in range(UNITS)]
-        weights = [work.tile([P, PIECE], F32, name="weight") for u in range(UNITS)]
-        totals = [work.tile([P, PIECE_QUERIES], F32, name="total") for u in range(UNITS)]
-        inverses = [work.tile([P, PIECE_QUERIES], F32, name="inverse") for u in range(UNITS)]
+        shifts = held.tile([P, BLOCKS], F32, name="shifts")
+        pres = [blocks.tile([P, TABLE], F32, name="pre") for b in range(BLOCKS)]
+        biases = [blocks.tile([P, TABLE], F32, name="bias") for b in range(BLOCKS)]
+        raws = [blocks.tile([P, PAIRS], F32, name="raw") for b in range(BLOCKS)]
+        scaleds = [blocks.tile([P, PAIRS], F32, name="scaled") for b in range(BLOCKS)]
+        logits = [blocks.tile([P, PAIRS], F32, name="logit") for b in range(BLOCKS)]
+        weights = [blocks.tile([P, PAIRS], F32, name="weight") for b in range(BLOCKS)]
+        minus_tops = [blocks.tile([P, QUERIES], F32, name="minus_top") for b in range(BLOCKS)]
+        totals = [blocks.tile([P, QUERIES], F32, name="total") for b in range(BLOCKS)]
+        inverses = [blocks.tile([P, QUERIES], F32, name="inverse") for b in range(BLOCKS)]
 
+        nc.sync.dma_start(shifts[:], b1.rearrange("(b p) o -> p (b o)", p=P))
         for b in range(BLOCKS):
-            nc.scalar.dma_start(shifts[b][:], b1[b * P : (b + 1) * P, :])
-        nc.sync.dma_start(pres[0][:], tab[0:P, :])
+            nc.sync.dma_start(pres[b][:], tab[heads_of(b), :])
         nc.sync.dma_start(offsets[:], offs)
-        nc.sync.dma_start(raws[0][:], dram_part(scores, 0))
-        nc.sync.dma_start(pres[1][:], tab[P : 2 * P, :])
-        for u in range(1, UNITS):
-            nc.sync.dma_start(raws[u][:], dram_part(scores, u))
+        for unit in UNITS:
+            nc.sync.dma_start(raws[unit[0]][:, pairs_of(unit)], scores[heads_of(unit[0]), pairs_of(unit)])
 
         warm = held.tile([P, 1], F32, name="warm")
         nc.vector.memset(warm[:], 0.0)
         warm_gelu = held.tile([P, 1], F32, name="warm_gelu")
         nc.scalar.activation(warm_gelu[:], warm[:], ACT.Gelu)
         for b in range(BLOCKS):
-            nc.scalar.activation(biases[b][:], pres[b][:], ACT.Gelu, bias=shifts[b][:])
+            nc.scalar.activation(biases[b][:], pres[b][:], ACT.Gelu, bias=shifts[:, b : b + 1])
         warm_exp = held.tile([P, 1], F32, name="warm_exp")
         nc.scalar.activation(warm_exp[:], biases[-1][:, 0:1], ACT.Exp)
 
-        def scale(u):
-            nc.vector.tensor_scalar_mul(scaleds[u][:], raws[u][:], SCALE)
+        def scale(unit):
+            b, pairs = unit[0], pairs_of(unit)
+            nc.vector.tensor_scalar_mul(scaleds[b][:, pairs], raws[b][:, pairs], SCALE)
 
-        def add_bias(u):
-            b, k = divmod(u, PIECES)
-            picked = biases[b][:].indirect(offsets[:, k * (PIECE // 16) : (k + 1) * (PIECE // 16)])
-            nc.vector.tensor_tensor(logits[u][:], picked, scaleds[u][:], ALU.add)
+        def add_bias(unit):
+            b, pairs = unit[0], pairs_of(unit)
+            picked = biases[b][:].indirect(offsets[:, pairs.start // 16 : pairs.stop // 16])
+            nc.vector.tensor_tensor(logits[b][:, pairs], picked, scaleds[b][:, pairs], ALU.add)
 
-        def exponentials(u):
+        def exponentials(unit):
+            b, first, n = unit
             nc.vector.tensor_reduce(
-                minus_tops[u][:], logits[u][:].rearrange("p (q k) -> p q k", k=KEYS), X, ALU.max, negate=True
+                minus_tops[b][:, queries_of(unit)], by_query(logits[b][:, pairs_of(unit)]), X, ALU.max, negate=True
             )
-            for q in range(PIECE_QUERIES):
+            for q in range(first, first + n):
                 keys = slice(q * KEYS, (q + 1) * KEYS)
                 nc.scalar.activation(
-                    weights[u][:, keys], logits[u][:, keys], ACT.Exp,
-                    bias=minus_tops[u][:, q : q + 1], accum_out=totals[u][:, q : q + 1],
+                    weights[b][:, keys], logits[b][:, keys], ACT.Exp,
+                    bias=minus_tops[b][:, q : q + 1], accum_out=totals[b][:, q : q + 1],
                 )
 
-        def invert(u):
-            nc.vector.reciprocal(inverses[u][:], totals[u][:])
+        def invert(unit):
+            b, queries = unit[0], queries_of(unit)
+            nc.vector.reciprocal(inverses[b][:, queries], totals[b][:, queries])
 
-        def divide(u):
-            by_query = weights[u][:].rearrange("p (q k) -> p q k", k=KEYS)
+        def divide(unit):
+            b, first, n = unit
+            pairs = pairs_of(unit)
             nc.vector.tensor_tensor(
-                by_query, by_query, inverses[u][:].unsqueeze(2).to_broadcast([P, PIECE_QUERIES, KEYS]), ALU.mult
+                by_query(weights[b][:, pairs]), by_query(weights[b][:, pairs]),
+                inverses[b][:, queries_of(unit)].unsqueeze(2).to_broadcast([P, n, KEYS]), ALU.mult,
             )
-            nc.sync.dma_start(dram_part(out, u), weights[u][:])
+            nc.sync.dma_start(out[heads_of(b), pairs], weights[b][:, pairs])
 
-        for u in range(AHEAD):
-            scale(u)
-        for u in range(UNITS):
-            add_bias(u)
-            if u + AHEAD < UNITS:
-                scale(u + AHEAD)
-            else:
-                invert(u - AHEAD)
-            exponentials(u)
-        for u in range(UNITS):
-            divide(u)
-            if u + AHEAD < UNITS:
-                invert(u + AHEAD)
+        scale(UNITS[0])
+        for unit, following in zip(UNITS, UNITS[1:] + [None]):
+            add_bias(unit)
+            if following:
+                scale(following)
+            exponentials(unit)
+        for unit in UNITS[:-1]:
+            invert(unit)
+        for unit in UNITS[:-1]:
+            divide(unit)
+        invert(UNITS[-1])
+        divide(UNITS[-1])

@@ -50,12 +50,13 @@ def tile_flexattentioncpb_kernel(tc, scores, tab, b1, offs, out):
         offsets = held.tile([P, PAIRS // 16], U16, name="offsets")
         shifts = held.tile([P, BLOCKS], F32, name="shifts")
         pres = [blocks.tile([P, TABLE], F32, name="pre") for b in range(BLOCKS)]
+        gelus = [blocks.tile([P, TABLE], F32, name="gelu") for b in range(BLOCKS)]
         biases = [blocks.tile([P, TABLE], F32, name="bias") for b in range(BLOCKS)]
         raws = [blocks.tile([P, PAIRS], F32, name="raw") for b in range(BLOCKS)]
-        scaleds = [blocks.tile([P, PAIRS], F32, name="scaled") for b in range(BLOCKS)]
         logits = [blocks.tile([P, PAIRS], F32, name="logit") for b in range(BLOCKS)]
         weights = [blocks.tile([P, PAIRS], F32, name="weight") for b in range(BLOCKS)]
         minus_tops = [blocks.tile([P, QUERIES], F32, name="minus_top") for b in range(BLOCKS)]
+        shifts_exp = [blocks.tile([P, QUERIES], F32, name="shift_exp") for b in range(BLOCKS)]
         totals = [blocks.tile([P, QUERIES], F32, name="total") for b in range(BLOCKS)]
         inverses = [blocks.tile([P, QUERIES], F32, name="inverse") for b in range(BLOCKS)]
 
@@ -71,29 +72,29 @@ def tile_flexattentioncpb_kernel(tc, scores, tab, b1, offs, out):
         warm_gelu = held.tile([P, 1], F32, name="warm_gelu")
         nc.scalar.activation(warm_gelu[:], warm[:], ACT.Gelu)
         for b in range(BLOCKS):
-            nc.scalar.activation(biases[b][:], pres[b][:], ACT.Gelu, bias=shifts[:, b : b + 1])
+            nc.scalar.activation(gelus[b][:], pres[b][:], ACT.Gelu, bias=shifts[:, b : b + 1])
         warm_exp = held.tile([P, 1], F32, name="warm_exp")
-        nc.scalar.activation(warm_exp[:], biases[-1][:, 0:1], ACT.Exp)
-
-        def scale(unit):
-            b, pairs = unit[0], pairs_of(unit)
-            nc.vector.tensor_scalar_mul(scaleds[b][:, pairs], raws[b][:, pairs], SCALE)
+        nc.scalar.activation(warm_exp[:], gelus[-1][:, 0:1], ACT.Exp)
 
         def add_bias(unit):
-            b, pairs = unit[0], pairs_of(unit)
+            b, first, n = unit
+            pairs = pairs_of(unit)
+            if first == 0:
+                nc.vector.tensor_scalar_mul(biases[b][:], gelus[b][:], 1.0 / SCALE)
             picked = biases[b][:].indirect(offsets[:, pairs.start // 16 : pairs.stop // 16])
-            nc.vector.tensor_tensor(logits[b][:, pairs], picked, scaleds[b][:, pairs], ALU.add)
+            nc.vector.tensor_tensor(logits[b][:, pairs], picked, raws[b][:, pairs], ALU.add)
 
         def exponentials(unit):
             b, first, n = unit
             nc.vector.tensor_reduce(
                 minus_tops[b][:, queries_of(unit)], by_query(logits[b][:, pairs_of(unit)]), X, ALU.max, negate=True
             )
+            nc.scalar.activation(shifts_exp[b][:, queries_of(unit)], minus_tops[b][:, queries_of(unit)], ACT.Copy, scale=SCALE)
             for q in range(first, first + n):
                 keys = slice(q * KEYS, (q + 1) * KEYS)
                 nc.scalar.activation(
-                    weights[b][:, keys], logits[b][:, keys], ACT.Exp,
-                    bias=minus_tops[b][:, q : q + 1], accum_out=totals[b][:, q : q + 1],
+                    weights[b][:, keys], logits[b][:, keys], ACT.Exp, scale=SCALE,
+                    bias=shifts_exp[b][:, q : q + 1], accum_out=totals[b][:, q : q + 1],
                 )
 
         def invert(unit):
@@ -109,11 +110,10 @@ def tile_flexattentioncpb_kernel(tc, scores, tab, b1, offs, out):
             )
             nc.sync.dma_start(out[heads_of(b), pairs], weights[b][:, pairs])
 
-        scale(UNITS[0])
+        add_bias(UNITS[0])
         for unit, following in zip(UNITS, UNITS[1:] + [None]):
-            add_bias(unit)
             if following:
-                scale(following)
+                add_bias(following)
             exponentials(unit)
         for unit in UNITS[:-1]:
             invert(unit)

@@ -73,14 +73,14 @@ def tile_flexattentioncpb_kernel(tc, scores, tab, b1, offs, out):
         nc.scalar.activation(warm_gelu[:], warm[:], ACT.Gelu)
         for b in range(BLOCKS):
             nc.scalar.activation(gelus[b][:], pres[b][:], ACT.Gelu, bias=shifts[:, b : b + 1])
+        nc.vector.tensor_scalar_mul(biases[0][:], gelus[0][:], 1.0 / SCALE)
+        for b in range(1, BLOCKS):
+            nc.scalar.activation(biases[b][:], gelus[b][:], ACT.Copy, scale=1.0 / SCALE)
         warm_exp = held.tile([P, 1], F32, name="warm_exp")
-        nc.scalar.activation(warm_exp[:], gelus[-1][:, 0:1], ACT.Exp)
+        nc.scalar.activation(warm_exp[:], biases[-1][:, 0:1], ACT.Exp)
 
         def add_bias(unit):
-            b, first, n = unit
-            pairs = pairs_of(unit)
-            if first == 0:
-                nc.vector.tensor_scalar_mul(biases[b][:], gelus[b][:], 1.0 / SCALE)
+            b, pairs = unit[0], pairs_of(unit)
             picked = biases[b][:].indirect(offsets[:, pairs.start // 16 : pairs.stop // 16])
             nc.vector.tensor_tensor(logits[b][:, pairs], picked, raws[b][:, pairs], ALU.add)
 

@@ -14,6 +14,7 @@ QUERIES = 32
 KEYS = 32
 PAIRS = QUERIES * KEYS
 SCALE = KEYS ** -0.5
+HALVES = [slice(0, TABLE // 2), slice(TABLE // 2, TABLE)]
 
 GROWING = (4, 12, 16)
 assert sum(GROWING) == QUERIES and max(GROWING) * KEYS <= TABLE
@@ -62,7 +63,8 @@ def tile_flexattentioncpb_kernel(tc, scores, tab, b1, offs, out):
 
         nc.sync.dma_start(shifts[:], b1.rearrange("(b p) o -> p (b o)", p=P))
         for b in range(BLOCKS):
-            nc.sync.dma_start(pres[b][:], tab[heads_of(b), :])
+            for half in HALVES:
+                nc.sync.dma_start(pres[b][:, half], tab[heads_of(b), half])
         nc.sync.dma_start(offsets[:], offs)
         for unit in UNITS:
             nc.sync.dma_start(raws[unit[0]][:, pairs_of(unit)], scores[heads_of(unit[0]), pairs_of(unit)])
@@ -72,8 +74,10 @@ def tile_flexattentioncpb_kernel(tc, scores, tab, b1, offs, out):
         warm_gelu = held.tile([P, 1], F32, name="warm_gelu")
         nc.scalar.activation(warm_gelu[:], warm[:], ACT.Gelu)
         for b in range(BLOCKS):
-            nc.scalar.activation(gelus[b][:], pres[b][:], ACT.Gelu, bias=shifts[:, b : b + 1])
-        nc.vector.tensor_scalar_mul(biases[0][:], gelus[0][:], 1.0 / SCALE)
+            for half in HALVES:
+                nc.scalar.activation(gelus[b][:, half], pres[b][:, half], ACT.Gelu, bias=shifts[:, b : b + 1])
+        for half in HALVES:
+            nc.vector.tensor_scalar_mul(biases[0][:, half], gelus[0][:, half], 1.0 / SCALE)
         for b in range(1, BLOCKS):
             nc.scalar.activation(biases[b][:], gelus[b][:], ACT.Copy, scale=1.0 / SCALE)
         warm_exp = held.tile([P, 1], F32, name="warm_exp")

import concourse.mybir as mybir

F32 = mybir.dt.float32
U16 = mybir.dt.uint16
ALU = mybir.AluOpType
ACT = mybir.ActivationFunctionType
X = mybir.AxisListType.X

P = 128
HEADS = 256
BLOCKS = HEADS // P
TABLE = 512
QUERIES = 32
KEYS = 32
PAIRS = QUERIES * KEYS
SCALE = KEYS ** -0.5
HALVES = [slice(0, TABLE // 2), slice(TABLE // 2, TABLE)]

GROWING = (4, 12, 16)
assert sum(GROWING) == QUERIES and max(GROWING) * KEYS <= TABLE


def units_of(block, sizes):
    return [(block, sum(sizes[:i]), n) for i, n in enumerate(sizes)]


UNITS = units_of(0, GROWING) + units_of(1, GROWING[::-1])


def tile_flexattentioncpb_kernel(tc, scores, tab, b1, offs, out):
    nc = tc.nc

    def pairs_of(unit):
        block, first, n = unit
        return slice(first * KEYS, (first + n) * KEYS)

    def queries_of(unit):
        block, first, n = unit
        return slice(first, first + n)

    def heads_of(block):
        return slice(block * P, (block + 1) * P)

    def by_query(columns):
        return columns.rearrange("p (q k) -> p q k", k=KEYS)

    with (
        tc.tile_pool(name="held", bufs=1) as held,
        tc.tile_pool(name="blocks", bufs=BLOCKS) as blocks,
    ):
        offsets = held.tile([P, PAIRS // 16], U16, name="offsets")
        shifts = held.tile([P, BLOCKS], F32, name="shifts")
        pres = [blocks.tile([P, TABLE], F32, name="pre") for b in range(BLOCKS)]
        gelus = [blocks.tile([P, TABLE], F32, name="gelu") for b in range(BLOCKS)]
        biases = [blocks.tile([P, TABLE], F32, name="bias") for b in range(BLOCKS)]
        raws = [blocks.tile([P, PAIRS], F32, name="raw") for b in range(BLOCKS)]
        logits = [blocks.tile([P, PAIRS], F32, name="logit") for b in range(BLOCKS)]
        weights = [blocks.tile([P, PAIRS], F32, name="weight") for b in range(BLOCKS)]
        minus_tops = [blocks.tile([P, QUERIES], F32, name="minus_top") for b in range(BLOCKS)]
        shifts_exp = [blocks.tile([P, QUERIES], F32, name="shift_exp") for b in range(BLOCKS)]
        totals = [blocks.tile([P, QUERIES], F32, name="total") for b in range(BLOCKS)]
        inverses = [blocks.tile([P, QUERIES], F32, name="inverse") for b in range(BLOCKS)]

        nc.sync.dma_start(shifts[:], b1.rearrange("(b p) o -> p (b o)", p=P))
        for b in range(BLOCKS):
            for half in HALVES:
                nc.sync.dma_start(pres[b][:, half], tab[heads_of(b), half])
        nc.sync.dma_start(offsets[:], offs)
        for unit in UNITS:
            nc.sync.dma_start(raws[unit[0]][:, pairs_of(unit)], scores[heads_of(unit[0]), pairs_of(unit)])

        warm = held.tile([P, 1], F32, name="warm")
        nc.vector.memset(warm[:], 0.0)
        warm_gelu = held.tile([P, 1], F32, name="warm_gelu")
        nc.scalar.activation(warm_gelu[:], warm[:], ACT.Gelu)
        for b in range(BLOCKS):
            for half in HALVES:
                nc.scalar.activation(gelus[b][:, half], pres[b][:, half], ACT.Gelu, bias=shifts[:, b : b + 1])
        for half in HALVES:
            nc.vector.tensor_scalar_mul(biases[0][:, half], gelus[0][:, half], 1.0 / SCALE)
        for b in range(1, BLOCKS):
            nc.scalar.activation(biases[b][:], gelus[b][:], ACT.Copy, scale=1.0 / SCALE)
        warm_exp = held.tile([P, 1], F32, name="warm_exp")
        nc.scalar.activation(warm_exp[:], biases[-1][:, 0:1], ACT.Exp)

        def add_bias(unit):
            b, pairs = unit[0], pairs_of(unit)
            picked = biases[b][:].indirect(offsets[:, pairs.start // 16 : pairs.stop // 16])
            nc.vector.tensor_tensor(logits[b][:, pairs], picked, raws[b][:, pairs], ALU.add)

        def exponentials(unit):
            b, first, n = unit
            nc.vector.tensor_reduce(
                minus_tops[b][:, queries_of(unit)], by_query(logits[b][:, pairs_of(unit)]), X, ALU.max, negate=True
            )
            nc.scalar.activation(shifts_exp[b][:, queries_of(unit)], minus_tops[b][:, queries_of(unit)], ACT.Copy, scale=SCALE)
            for q in range(first, first + n):
                keys = slice(q * KEYS, (q + 1) * KEYS)
                nc.scalar.activation(
                    weights[b][:, keys], logits[b][:, keys], ACT.Exp, scale=SCALE,
                    bias=shifts_exp[b][:, q : q + 1], accum_out=totals[b][:, q : q + 1],
                )

        def invert(unit):
            b, queries = unit[0], queries_of(unit)
            nc.vector.reciprocal(inverses[b][:, queries], totals[b][:, queries])

        def divide(unit):
            b, first, n = unit
            pairs = pairs_of(unit)
            nc.vector.tensor_tensor(
                by_query(weights[b][:, pairs]), by_query(weights[b][:, pairs]),
                inverses[b][:, queries_of(unit)].unsqueeze(2).to_broadcast([P, n, KEYS]), ALU.mult,
            )
            nc.sync.dma_start(out[heads_of(b), pairs], weights[b][:, pairs])

        add_bias(UNITS[0])
        for unit, following in zip(UNITS, UNITS[1:] + [None]):
            if following:
                add_bias(following)
            exponentials(unit)
        for unit in UNITS[:-1]:
            invert(unit)
        for unit in UNITS[:-1]:
            divide(unit)
        invert(UNITS[-1])
        divide(UNITS[-1])
